import numpy as np
import ml_dtypes


BF16 = ml_dtypes.bfloat16


def bf(x):
    return np.asarray(x, np.float32).astype(BF16)


def f64(x):
    return np.asarray(x).astype(np.float64)


E2M1 = np.array([0.0, 0.5, 1.0, 1.5, 2.0, 3.0, 4.0, 6.0, -0.0, -0.5, -1.0, -1.5, -2.0, -3.0, -4.0, -6.0])


def pack_weight(w, fmt):
    k, n = w.shape
    w = f64(bf(w)).reshape(k // 32, 32, n)
    amax = np.abs(w).max(1)
    if fmt == "e4m3":
        byte = np.frexp(amax)[1] - 1 + 127 - 7
    else:
        mant, ex = np.frexp(amax / 6.0)
        byte = np.where(mant > 0.5, ex, ex - 1) + 127
    byte = np.clip(np.where(amax > 0, byte, 1), 1, 254)
    scaled = (w * np.exp2(127.0 - byte)[:, None, :]).reshape(k, n).astype(np.float32)
    by_word = np.ascontiguousarray(scaled.reshape(k // 512, 128, 4, n).transpose(0, 1, 3, 2))
    if fmt == "e4m3":
        words = by_word.astype(ml_dtypes.float8_e4m3fn).view(np.uint8)
    else:
        c = by_word.astype(ml_dtypes.float4_e2m1fn).view(np.uint8) & 0xF
        words = c[..., 0::2] | (c[..., 1::2] << 4)
    return np.ascontiguousarray(words), np.ascontiguousarray(byte.astype(np.uint8).reshape(k // 512, 16, n))


def unpack_weight(words, scales, fmt):
    g, p, n, _ = words.shape
    if fmt == "e4m3":
        vals = np.ascontiguousarray(words).view(ml_dtypes.float8_e4m3fn).astype(np.float64)
    else:
        nib = np.empty((g, p, n, 4), np.uint8)
        nib[..., 0::2] = words & 0xF
        nib[..., 1::2] = words >> 4
        vals = E2M1[nib]
    vals = vals * np.repeat(np.exp2(scales.astype(np.float64) - 127.0), 8, axis=1)[..., None]
    return vals.transpose(0, 1, 3, 2).reshape(g * 512, n)

def pack4(w):
    words, scales = pack_weight(w, "e2m1")
    return words.reshape(words.shape[0], 128, -1), scales


def unpack4(words, scales):
    return unpack_weight(words.reshape(words.shape[0], 128, -1, 2), scales, "e2m1")


def kspread(k):
    return np.exp2(np.repeat(np.random.randint(-6, 7, k // 32), 32).astype(np.float64))


B, S, HID, NH, NOPE, ROPE, VD, KV_RANK, SW, QB = 1, 2048, 8192, 8, 64, 128, 128, 512, 384, 128
QK = NOPE + ROPE


def rotate_half(x):
    h = x.shape[-1] // 2
    return np.concatenate([-x[..., h:], x[..., :h]], axis=-1)


def rope_tables():
    pos = np.arange(S, dtype=np.float64)
    inv = 1.0 / (10000.0 ** (np.arange(0, ROPE, 2, dtype=np.float64) / ROPE))
    ang = pos[:, None] * inv[None, :]
    ang = np.concatenate([ang, ang], axis=-1)
    return bf(np.broadcast_to(np.cos(ang)[None], (B, S, ROPE))), bf(np.broadcast_to(np.sin(ang)[None], (B, S, ROPE)))


def setup_inputs():
    s = kspread(HID)
    cos, sin = rope_tables()
    hidden_states = np.random.standard_normal((B, S, HID)) * s
    hidden_states_words, hidden_states_scales = pack4(hidden_states.reshape(B * S, HID).T)
    Wq_words, Wq_scales = pack4(np.random.standard_normal((HID, NH * QK)) * 2.0 / np.sqrt(HID) / s[:, None])
    bq = bf(np.random.standard_normal(NH * QK) * 0.2)
    return {"hidden_states_words": hidden_states_words, "hidden_states_scales": hidden_states_scales, "cos": cos, "sin": sin,
            "Wq_words": Wq_words, "Wq_scales": Wq_scales,
            "bq": bq}


def reference(hidden_states_words, hidden_states_scales, cos, sin, Wq_words, Wq_scales, bq):
    q = ((unpack4(hidden_states_words, hidden_states_scales).T.reshape(B, S, HID) @ unpack4(Wq_words, Wq_scales)) + f64(bq)).reshape(B, S, NH, QK).transpose(0, 2, 1, 3)
    q_nope, q_rope = q[..., :NOPE], q[..., NOPE:]
    c, si = f64(cos)[:, None], f64(sin)[:, None]
    q_rope = q_rope * c + rotate_half(q_rope) * si
    return np.concatenate([q_nope, q_rope], axis=-1)

@@ -1,0 +1,213 @@
+from contextlib import ExitStack
+
+import concourse.mybir as mybir
+
+F32 = mybir.dt.float32
+BF16 = mybir.dt.bfloat16
+I32 = mybir.dt.int32
+U8 = mybir.dt.uint8
+FP4X4 = mybir.dt.float4_e2m1fn_x4
+ADD = mybir.AluOpType.add
+MULT = mybir.AluOpType.mult
+
+P = 128
+PASSES = 16
+TOKENS = 2048
+CHANNELS = 1536
+HEADS = 8
+HEAD = 192
+NOPE = 64
+ROPE = 128
+HALF = 64
+M_TILES = TOKENS // P
+BANK = 512
+
+FLOPS = 2 * TOKENS * 8192 * CHANNELS
+
+WARM = 10
+FIRST_M = 4
+FIRST_COLS = 1024
+RUNS = (1, 3, 4, 4, 4)
+
+
+def tile_gptossmlaattention_pb_kernel(
+    tc, hidden_states_words, hidden_states_scales, cos, sin, Wq_words, Wq_scales, bq, out
+):
+    nc = tc.nc
+    with ExitStack() as ctx:
+        keep = ctx.enter_context(tc.tile_pool(name="keep", bufs=1))
+        work = ctx.enter_context(tc.tile_pool(name="work", bufs=5))
+        temp = ctx.enter_context(tc.tile_pool(name="temp", bufs=2))
+        psum = ctx.enter_context(tc.psum_pool(name="psum", bufs=8))
+        ctx.enter_context(tc.manual_schedule())
+
+        x_codes = {}
+        x_scale = {}
+        w_codes = {}
+        w_scale = {}
+
+        def load_codes(table, src, g0, npass, c0, ncols, name):
+            t = keep.tile([P, npass, 2 * ncols], U8, name=name, align_bytes=64)
+            nc.sync.dma_start(
+                out=t[:].bitcast(I32),
+                in_=src[g0 : g0 + npass, :, 2 * c0 : 2 * (c0 + ncols)].rearrange("g p b -> p g b").bitcast(I32),
+            )
+            for j in range(npass):
+                table[(c0, g0 + j)] = t[:, j, :]
+
+        def load_scales(table, src, g0, npass, c0, ncols, name):
+            t = keep.tile([P, npass, ncols], U8, name=name, align_bytes=64)
+            nc.vector.memset(t[:].bitcast(I32), 0)
+            for q in range(4):
+                nc.sync.dma_start(
+                    out=t[32 * q : 32 * q + 4, :, :].bitcast(I32),
+                    in_=src[g0 : g0 + npass, 4 * q : 4 * q + 4, c0 : c0 + ncols].rearrange("g r n -> r g n").bitcast(I32),
+                )
+            for j in range(npass):
+                table[(c0, g0 + j)] = t[:, j, :]
+
+        warm = keep.tile([P, BANK], BF16, name="warm")
+        nc.gpsimd.memset(warm[:], 0.0)
+
+        first_tok = FIRST_M * P
+        g0 = 0
+        for r, npass in enumerate(RUNS):
+            if r == 0:
+                load_codes(w_codes, Wq_words, 0, 1, 0, FIRST_COLS, "wa0")
+                load_codes(x_codes, hidden_states_words, 0, 1, 0, first_tok, "xa0")
+            load_scales(x_scale, hidden_states_scales, g0, npass, 0, first_tok, "xsa%d" % r)
+            load_scales(w_scale, Wq_scales, g0, npass, 0, FIRST_COLS, "wsa%d" % r)
+            for g in range(g0, g0 + npass):
+                if g > 0:
+                    load_codes(w_codes, Wq_words, g, 1, 0, FIRST_COLS, "wa%d" % g)
+                    load_codes(x_codes, hidden_states_words, g, 1, 0, first_tok, "xa%d" % g)
+            g0 += npass
+
+        bias = keep.tile([P, CHANNELS], BF16, name="bias")
+        nc.sync.dma_start(out=bias[:], in_=bq.partition_broadcast(P))
+
+        load_scales(w_scale, Wq_scales, 0, PASSES, FIRST_COLS, CHANNELS - FIRST_COLS, "wsb")
+        for g in range(0, PASSES, 4):
+            load_codes(w_codes, Wq_words, g, 4, FIRST_COLS, CHANNELS - FIRST_COLS, "wb%d" % g)
+
+        cos_t = keep.tile([P, M_TILES, ROPE], BF16, name="cos_t")
+        sin_t = keep.tile([P, M_TILES, ROPE], BF16, name="sin_t")
+        nc.sync.dma_start(out=cos_t[:], in_=cos[0].rearrange("(m p) d -> p m d", p=P))
+        nc.sync.dma_start(out=sin_t[:], in_=sin[0].rearrange("(m p) d -> p m d", p=P))
+
+        load_scales(x_scale, hidden_states_scales, 0, PASSES, 512, 512, "xsb")
+        for g in range(0, PASSES, 4):
+            load_codes(x_codes, hidden_states_words, g, 4, 512, 512, "xb%d" % g)
+        load_scales(x_scale, hidden_states_scales, 0, PASSES, 1024, 1024, "xsc")
+        for g in range(0, PASSES, 2):
+            load_codes(x_codes, hidden_states_words, g, 2, 1024, 1024, "xc%d" % g)
+
+        def x_block(m):
+            tok = m * P
+            if tok < 512:
+                return 0
+            if tok < 1024:
+                return 512
+            return 1024
+
+        def mm(acc, m, c0, width, g):
+            xb = x_block(m)
+            xo = m * P - xb
+            wb = 0 if c0 < FIRST_COLS else FIRST_COLS
+            wo = c0 - wb
+            nc.tensor.matmul_mx(
+                out=acc[:, 0:width],
+                lhsT=x_codes[(xb, g)][:, 2 * xo : 2 * (xo + P)].bitcast(FP4X4),
+                lhsT_scale=x_scale[(xb, g)][:, xo : xo + P],
+                rhs=w_codes[(wb, g)][:, 2 * wo : 2 * (wo + width)].bitcast(FP4X4),
+                rhs_scale=w_scale[(wb, g)][:, wo : wo + width],
+                start=(g == 0),
+                stop=(g == PASSES - 1),
+            )
+
+        def evacuate(res, acc, c0, width):
+            nc.vector.tensor_tensor(
+                out=res[:, c0 : c0 + width], in0=acc[:, 0:width], in1=bias[:, c0 : c0 + width], op=ADD
+            )
+
+        def spread(table, m, d0, d1, nh):
+            return table[:, m, d0:d1].unsqueeze(1).to_broadcast([P, nh, d1 - d0])
+
+        def rope(res, m, h0, h1):
+            nh = h1 - h0
+            res3 = res[:].rearrange("p (h d) -> p h d", h=HEADS)
+            tmp = temp.tile([P, HEADS, ROPE], F32, name="tmp")
+            nc.vector.tensor_tensor(
+                out=tmp[:, h0:h1, 0:HALF], in0=res3[:, h0:h1, NOPE + HALF : HEAD],
+                in1=spread(sin_t, m, 0, HALF, nh), op=MULT,
+            )
+            nc.vector.tensor_tensor(
+                out=tmp[:, h0:h1, HALF:ROPE], in0=res3[:, h0:h1, NOPE : NOPE + HALF],
+                in1=spread(sin_t, m, HALF, ROPE, nh), op=MULT,
+            )
+            nc.vector.tensor_tensor(
+                out=res3[:, h0:h1, NOPE:HEAD], in0=res3[:, h0:h1, NOPE:HEAD],
+                in1=spread(cos_t, m, 0, ROPE, nh), op=MULT,
+            )
+            nc.vector.tensor_tensor(
+                out=res3[:, h0:h1, NOPE:HEAD], in0=res3[:, h0:h1, NOPE:HEAD], in1=tmp[:, h0:h1, :], op=ADD
+            )
+
+        def store(queue, res, m, h0, h1):
+            res3 = res[:].rearrange("p (h d) -> p h d", h=HEADS)
+            queue.dma_start(
+                out=out[0, h0:h1, m * P : (m + 1) * P, :].rearrange("h p d -> p h d"), in_=res3[:, h0:h1, :]
+            )
+
+        dummy = psum.tile([P, BANK], F32, name="acc")
+        for i in range(WARM):
+            nc.tensor.matmul(out=dummy[:], lhsT=warm[:, 0:P], rhs=warm[:], start=True, stop=True)
+
+        accs = {}
+        ress = {}
+        for m in range(FIRST_M):
+            for n in range(2):
+                acc = psum.tile([P, BANK], F32, name="acc")
+                accs[(m, n)] = acc
+        for g in range(PASSES):
+            for m in range(FIRST_M):
+                for n in range(2):
+                    mm(accs[(m, n)], m, n * BANK, BANK, g)
+        for m in range(FIRST_M):
+            res = work.tile([P, CHANNELS], F32, name="res")
+            ress[m] = res
+            for n in range(2):
+                evacuate(res, accs[(m, n)], n * BANK, BANK)
+
+        nc.vector.tensor_scalar(
+            out=sin_t[:, :, 0:HALF], in0=sin_t[:, :, 0:HALF], scalar1=-1.0, scalar2=None, op0=MULT
+        )
+
+        for m in range(FIRST_M):
+            acc = psum.tile([P, BANK], F32, name="acc")
+            for g in range(PASSES):
+                mm(acc, m, 2 * BANK, BANK, g)
+            evacuate(ress[m], acc, 2 * BANK, BANK)
+            rope(ress[m], m, 0, HEADS)
+            store(nc.scalar, ress[m], m, 0, HEADS)
+
+        for m in range(FIRST_M, M_TILES - 1):
+            res = work.tile([P, CHANNELS], F32, name="res")
+            for n in range(3):
+                acc = psum.tile([P, BANK], F32, name="acc")
+                for g in range(PASSES):
+                    mm(acc, m, n * BANK, BANK, g)
+                evacuate(res, acc, n * BANK, BANK)
+            rope(res, m, 0, HEADS)
+            store(nc.scalar, res, m, 0, HEADS)
+
+        m = M_TILES - 1
+        res = work.tile([P, CHANNELS], F32, name="res")
+        tail = ((0, 512, 0, 2), (512, 512, 2, 5), (1024, 256, 5, 6), (1280, 128, 6, 7), (1408, 128, 7, 8))
+        for i, (c0, width, h0, h1) in enumerate(tail):
+            acc = psum.tile([P, BANK], F32, name="acc")
+            for g in range(PASSES):
+                mm(acc, m, c0, width, g)
+            evacuate(res, acc, c0, width)
+            rope(res, m, h0, h1)
+            store(nc.sync if i % 2 else nc.scalar, res, m, h0, h1)

@@ -21,13 +21,12 @@ ROPE = 128
 HALF = 64
 M_TILES = TOKENS // P
 BANK = 512
+SCALE_ROWS = 256
 
 FLOPS = 2 * TOKENS * 8192 * CHANNELS
 
-WARM = 10
+WARM = 4
 FIRST_M = 4
-FIRST_COLS = 1024
-RUNS = (1, 3, 4, 4, 4)
 
 
 def tile_gptossmlaattention_pb_kernel(
@@ -41,88 +40,75 @@ def tile_gptossmlaattention_pb_kernel(
         psum = ctx.enter_context(tc.psum_pool(name="psum", bufs=8))
         ctx.enter_context(tc.manual_schedule())
 
-        x_codes = {}
-        x_scale = {}
-        w_codes = {}
-        w_scale = {}
+        x_rows = hidden_states_scales.rearrange("g q n -> (g q) n")
+        w_rows = Wq_scales.rearrange("g q n -> (g q) n")
+        x_table = [[] for v in range(PASSES)]
+        w_table = [[] for v in range(PASSES)]
 
-        def load_codes(table, src, g0, npass, c0, ncols, name):
-            t = keep.tile([P, npass, 2 * ncols], U8, name=name, align_bytes=64)
+        def load(table, words, rows, v, c0, ncols, name):
+            u = v // 8
+            s = v % 8
+            g = 8 * u + s // 4
+            p0 = 32 * (s % 4)
+            codes = keep.tile([P, 2 * ncols], U8, name="%sc%d" % (name, v), align_bytes=64)
             nc.sync.dma_start(
-                out=t[:].bitcast(I32),
-                in_=src[g0 : g0 + npass, :, 2 * c0 : 2 * (c0 + ncols)].rearrange("g p b -> p g b").bitcast(I32),
+                out=codes[:].bitcast(I32),
+                in_=words[g : g + 7 : 2, p0 : p0 + 32, 2 * c0 : 2 * (c0 + ncols)].bitcast(I32),
             )
-            for j in range(npass):
-                table[(c0, g0 + j)] = t[:, j, :]
+            plane = keep.tile([P, ncols], U8, name="%ss%d" % (name, v), align_bytes=64)
+            r0 = 128 * u + 4 * s
+            nrows = min(P, SCALE_ROWS - r0)
+            if nrows < P:
+                nc.vector.memset(plane[96:P, :].bitcast(I32), 0)
+            nc.sync.dma_start(
+                out=plane[0:nrows, :].bitcast(I32), in_=rows[r0 : r0 + nrows, c0 : c0 + ncols].bitcast(I32)
+            )
+            table[v].append((c0, c0 + ncols, codes, plane))
 
-        def load_scales(table, src, g0, npass, c0, ncols, name):
-            t = keep.tile([P, npass, ncols], U8, name=name, align_bytes=64)
-            nc.vector.memset(t[:].bitcast(I32), 0)
-            for q in range(4):
-                nc.sync.dma_start(
-                    out=t[32 * q : 32 * q + 4, :, :].bitcast(I32),
-                    in_=src[g0 : g0 + npass, 4 * q : 4 * q + 4, c0 : c0 + ncols].rearrange("g r n -> r g n").bitcast(I32),
-                )
-            for j in range(npass):
-                table[(c0, g0 + j)] = t[:, j, :]
+        def operand(table, v, c0, width):
+            for a, b, codes, plane in table[v]:
+                if a <= c0 and c0 + width <= b:
+                    return codes[:, 2 * (c0 - a) : 2 * (c0 - a + width)], plane[:, c0 - a : c0 - a + width]
+            return None
 
         warm = keep.tile([P, BANK], BF16, name="warm")
-        nc.gpsimd.memset(warm[:], 0.0)
+        nc.vector.memset(warm[:], 0.0)
 
         first_tok = FIRST_M * P
-        g0 = 0
-        for r, npass in enumerate(RUNS):
-            if r == 0:
-                load_codes(w_codes, Wq_words, 0, 1, 0, FIRST_COLS, "wa0")
-                load_codes(x_codes, hidden_states_words, 0, 1, 0, first_tok, "xa0")
-            load_scales(x_scale, hidden_states_scales, g0, npass, 0, first_tok, "xsa%d" % r)
-            load_scales(w_scale, Wq_scales, g0, npass, 0, FIRST_COLS, "wsa%d" % r)
-            for g in range(g0, g0 + npass):
-                if g > 0:
-                    load_codes(w_codes, Wq_words, g, 1, 0, FIRST_COLS, "wa%d" % g)
-                    load_codes(x_codes, hidden_states_words, g, 1, 0, first_tok, "xa%d" % g)
-            g0 += npass
+        load(x_table, hidden_states_words, x_rows, 0, 0, first_tok, "xa")
+        load(w_table, Wq_words, w_rows, 0, 0, BANK, "wa")
+        load(w_table, Wq_words, w_rows, 0, BANK, BANK, "wz")
+        for v in range(1, PASSES):
+            load(x_table, hidden_states_words, x_rows, v, 0, first_tok, "xa")
+            load(w_table, Wq_words, w_rows, v, 0, 2 * BANK, "wa")
 
         bias = keep.tile([P, CHANNELS], BF16, name="bias")
         nc.sync.dma_start(out=bias[:], in_=bq.partition_broadcast(P))
 
-        load_scales(w_scale, Wq_scales, 0, PASSES, FIRST_COLS, CHANNELS - FIRST_COLS, "wsb")
-        for g in range(0, PASSES, 4):
-            load_codes(w_codes, Wq_words, g, 4, FIRST_COLS, CHANNELS - FIRST_COLS, "wb%d" % g)
+        for v in range(PASSES):
+            load(w_table, Wq_words, w_rows, v, 2 * BANK, BANK, "wb")
+        for v in range(PASSES):
+            load(x_table, hidden_states_words, x_rows, v, 512, 512, "xb")
 
         cos_t = keep.tile([P, M_TILES, ROPE], BF16, name="cos_t")
         sin_t = keep.tile([P, M_TILES, ROPE], BF16, name="sin_t")
         nc.sync.dma_start(out=cos_t[:], in_=cos[0].rearrange("(m p) d -> p m d", p=P))
         nc.sync.dma_start(out=sin_t[:], in_=sin[0].rearrange("(m p) d -> p m d", p=P))
 
-        load_scales(x_scale, hidden_states_scales, 0, PASSES, 512, 512, "xsb")
-        for g in range(0, PASSES, 4):
-            load_codes(x_codes, hidden_states_words, g, 4, 512, 512, "xb%d" % g)
-        load_scales(x_scale, hidden_states_scales, 0, PASSES, 1024, 1024, "xsc")
-        for g in range(0, PASSES, 2):
-            load_codes(x_codes, hidden_states_words, g, 2, 1024, 1024, "xc%d" % g)
+        for v in range(PASSES):
+            load(x_table, hidden_states_words, x_rows, v, 1024, 1024, "xc")
 
-        def x_block(m):
-            tok = m * P
-            if tok < 512:
-                return 0
-            if tok < 1024:
-                return 512
-            return 1024
-
-        def mm(acc, m, c0, width, g):
-            xb = x_block(m)
-            xo = m * P - xb
-            wb = 0 if c0 < FIRST_COLS else FIRST_COLS
-            wo = c0 - wb
+        def mm(acc, m, c0, width, v):
+            xc, xs = operand(x_table, v, m * P, P)
+            wc, ws = operand(w_table, v, c0, width)
             nc.tensor.matmul_mx(
                 out=acc[:, 0:width],
-                lhsT=x_codes[(xb, g)][:, 2 * xo : 2 * (xo + P)].bitcast(FP4X4),
-                lhsT_scale=x_scale[(xb, g)][:, xo : xo + P],
-                rhs=w_codes[(wb, g)][:, 2 * wo : 2 * (wo + width)].bitcast(FP4X4),
-                rhs_scale=w_scale[(wb, g)][:, wo : wo + width],
-                start=(g == 0),
-                stop=(g == PASSES - 1),
+                lhsT=xc.bitcast(FP4X4),
+                lhsT_scale=xs,
+                rhs=wc.bitcast(FP4X4),
+                rhs_scale=ws,
+                start=(v == 0),
+                stop=(v == PASSES - 1),
             )
 
         def evacuate(res, acc, c0, width):
@@ -165,29 +151,34 @@ def tile_gptossmlaattention_pb_kernel(
 
         accs = {}
         ress = {}
-        for m in range(FIRST_M):
-            for n in range(2):
+        for n in range(2):
+            for m in range(FIRST_M):
                 acc = psum.tile([P, BANK], F32, name="acc")
                 accs[(m, n)] = acc
-        for g in range(PASSES):
-            for m in range(FIRST_M):
-                for n in range(2):
-                    mm(accs[(m, n)], m, n * BANK, BANK, g)
+        for v in range(PASSES):
+            for n in range(2):
+                for m in range(FIRST_M):
+                    mm(accs[(m, n)], m, n * BANK, BANK, v)
         for m in range(FIRST_M):
             res = work.tile([P, CHANNELS], F32, name="res")
             ress[m] = res
-            for n in range(2):
-                evacuate(res, accs[(m, n)], n * BANK, BANK)
+        for n in range(2):
+            for m in range(FIRST_M):
+                evacuate(ress[m], accs[(m, n)], n * BANK, BANK)
+
+        for m in range(FIRST_M):
+            acc = psum.tile([P, BANK], F32, name="acc")
+            accs[(m, 2)] = acc
+        for v in range(PASSES):
+            for m in range(FIRST_M):
+                mm(accs[(m, 2)], m, 2 * BANK, BANK, v)
+        for m in range(FIRST_M):
+            evacuate(ress[m], accs[(m, 2)], 2 * BANK, BANK)
 
         nc.vector.tensor_scalar(
             out=sin_t[:, :, 0:HALF], in0=sin_t[:, :, 0:HALF], scalar1=-1.0, scalar2=None, op0=MULT
         )
-
         for m in range(FIRST_M):
-            acc = psum.tile([P, BANK], F32, name="acc")
-            for g in range(PASSES):
-                mm(acc, m, 2 * BANK, BANK, g)
-            evacuate(ress[m], acc, 2 * BANK, BANK)
             rope(ress[m], m, 0, HEADS)
             store(nc.scalar, ress[m], m, 0, HEADS)
 
@@ -195,19 +186,21 @@ def tile_gptossmlaattention_pb_kernel(
             res = work.tile([P, CHANNELS], F32, name="res")
             for n in range(3):
                 acc = psum.tile([P, BANK], F32, name="acc")
-                for g in range(PASSES):
-                    mm(acc, m, n * BANK, BANK, g)
+                for v in range(PASSES):
+                    mm(acc, m, n * BANK, BANK, v)
                 evacuate(res, acc, n * BANK, BANK)
             rope(res, m, 0, HEADS)
             store(nc.scalar, res, m, 0, HEADS)
 
         m = M_TILES - 1
         res = work.tile([P, CHANNELS], F32, name="res")
-        tail = ((0, 512, 0, 2), (512, 512, 2, 5), (1024, 256, 5, 6), (1280, 128, 6, 7), (1408, 128, 7, 8))
+        tail = (
+            (0, 512, 0, 2), (512, 256, 2, 4), (768, 256, 4, 5), (1024, 128, 5, 6), (1152, 256, 6, 7), (1408, 128, 7, 8),
+        )
         for i, (c0, width, h0, h1) in enumerate(tail):
             acc = psum.tile([P, BANK], F32, name="acc")
-            for g in range(PASSES):
-                mm(acc, m, c0, width, g)
+            for v in range(PASSES):
+                mm(acc, m, c0, width, v)
             evacuate(res, acc, c0, width)
             rope(res, m, h0, h1)
             store(nc.sync if i % 2 else nc.scalar, res, m, h0, h1)

@@ -21,12 +21,12 @@ ROPE = 128
 HALF = 64
 M_TILES = TOKENS // P
 BANK = 512
-SCALE_ROWS = 256
 
 FLOPS = 2 * TOKENS * 8192 * CHANNELS
 
-WARM = 4
+WARM = 10
 FIRST_M = 4
+RUNS = (1, 3, 4, 4, 4)
 
 
 def tile_gptossmlaattention_pb_kernel(
@@ -40,75 +40,81 @@ def tile_gptossmlaattention_pb_kernel(
         psum = ctx.enter_context(tc.psum_pool(name="psum", bufs=8))
         ctx.enter_context(tc.manual_schedule())
 
-        x_rows = hidden_states_scales.rearrange("g q n -> (g q) n")
-        w_rows = Wq_scales.rearrange("g q n -> (g q) n")
-        x_table = [[] for v in range(PASSES)]
-        w_table = [[] for v in range(PASSES)]
+        x_codes = [[] for g in range(PASSES)]
+        x_scale = [[] for g in range(PASSES)]
+        w_codes = [[] for g in range(PASSES)]
+        w_scale = [[] for g in range(PASSES)]
 
-        def load(table, words, rows, v, c0, ncols, name):
-            u = v // 8
-            s = v % 8
-            g = 8 * u + s // 4
-            p0 = 32 * (s % 4)
-            codes = keep.tile([P, 2 * ncols], U8, name="%sc%d" % (name, v), align_bytes=64)
+        def load_codes(table, src, g0, npass, c0, ncols, name):
+            t = keep.tile([P, npass, 2 * ncols], U8, name=name, align_bytes=64)
             nc.sync.dma_start(
-                out=codes[:].bitcast(I32),
-                in_=words[g : g + 7 : 2, p0 : p0 + 32, 2 * c0 : 2 * (c0 + ncols)].bitcast(I32),
+                out=t[:].bitcast(I32),
+                in_=src[g0 : g0 + npass, :, 2 * c0 : 2 * (c0 + ncols)].rearrange("g p b -> p g b").bitcast(I32),
             )
-            plane = keep.tile([P, ncols], U8, name="%ss%d" % (name, v), align_bytes=64)
-            r0 = 128 * u + 4 * s
-            nrows = min(P, SCALE_ROWS - r0)
-            if nrows < P:
-                nc.vector.memset(plane[96:P, :].bitcast(I32), 0)
-            nc.sync.dma_start(
-                out=plane[0:nrows, :].bitcast(I32), in_=rows[r0 : r0 + nrows, c0 : c0 + ncols].bitcast(I32)
-            )
-            table[v].append((c0, c0 + ncols, codes, plane))
+            for j in range(npass):
+                table[g0 + j].append((c0, c0 + ncols, t[:, j, :]))
 
-        def operand(table, v, c0, width):
-            for a, b, codes, plane in table[v]:
+        def load_scales(table, src, g0, npass, c0, ncols, name):
+            t = keep.tile([P, npass, ncols], U8, name=name, align_bytes=64)
+            nc.vector.memset(t[:].bitcast(I32), 0)
+            for q in range(4):
+                nc.sync.dma_start(
+                    out=t[32 * q : 32 * q + 4, :, :].bitcast(I32),
+                    in_=src[g0 : g0 + npass, 4 * q : 4 * q + 4, c0 : c0 + ncols].rearrange("g r n -> r g n").bitcast(I32),
+                )
+            for j in range(npass):
+                table[g0 + j].append((c0, c0 + ncols, t[:, j, :]))
+
+        def window(table, g, c0, width, unit):
+            for a, b, t in table[g]:
                 if a <= c0 and c0 + width <= b:
-                    return codes[:, 2 * (c0 - a) : 2 * (c0 - a + width)], plane[:, c0 - a : c0 - a + width]
+                    return t[:, unit * (c0 - a) : unit * (c0 - a + width)]
             return None
 
         warm = keep.tile([P, BANK], BF16, name="warm")
-        nc.vector.memset(warm[:], 0.0)
+        nc.gpsimd.memset(warm[:], 0.0)
 
         first_tok = FIRST_M * P
-        load(x_table, hidden_states_words, x_rows, 0, 0, first_tok, "xa")
-        load(w_table, Wq_words, w_rows, 0, 0, BANK, "wa")
-        load(w_table, Wq_words, w_rows, 0, BANK, BANK, "wz")
-        for v in range(1, PASSES):
-            load(x_table, hidden_states_words, x_rows, v, 0, first_tok, "xa")
-            load(w_table, Wq_words, w_rows, v, 0, 2 * BANK, "wa")
+        g0 = 0
+        for r, npass in enumerate(RUNS):
+            if r == 0:
+                load_codes(w_codes, Wq_words, 0, 1, 0, 2 * BANK, "wa0")
+                load_codes(x_codes, hidden_states_words, 0, 1, 0, first_tok, "xa0")
+            load_scales(x_scale, hidden_states_scales, g0, npass, 0, first_tok, "xsa%d" % r)
+            load_scales(w_scale, Wq_scales, g0, npass, 0, 2 * BANK, "wsa%d" % r)
+            for g in range(max(g0, 1), g0 + npass):
+                load_codes(w_codes, Wq_words, g, 1, 0, 2 * BANK, "wa%d" % g)
+                load_codes(x_codes, hidden_states_words, g, 1, 0, first_tok, "xa%d" % g)
+            g0 += npass
 
         bias = keep.tile([P, CHANNELS], BF16, name="bias")
         nc.sync.dma_start(out=bias[:], in_=bq.partition_broadcast(P))
 
-        for v in range(PASSES):
-            load(w_table, Wq_words, w_rows, v, 2 * BANK, BANK, "wb")
-        for v in range(PASSES):
-            load(x_table, hidden_states_words, x_rows, v, 512, 512, "xb")
+        load_scales(w_scale, Wq_scales, 0, PASSES, 2 * BANK, BANK, "wsb")
+        load_scales(x_scale, hidden_states_scales, 0, PASSES, 512, 512, "xsb")
+        for g in range(0, PASSES, 4):
+            load_codes(w_codes, Wq_words, g, 4, 2 * BANK, BANK, "wb%d" % g)
+        for g in range(0, PASSES, 4):
+            load_codes(x_codes, hidden_states_words, g, 4, 512, 512, "xb%d" % g)
 
         cos_t = keep.tile([P, M_TILES, ROPE], BF16, name="cos_t")
         sin_t = keep.tile([P, M_TILES, ROPE], BF16, name="sin_t")
         nc.sync.dma_start(out=cos_t[:], in_=cos[0].rearrange("(m p) d -> p m d", p=P))
         nc.sync.dma_start(out=sin_t[:], in_=sin[0].rearrange("(m p) d -> p m d", p=P))
 
-        for v in range(PASSES):
-            load(x_table, hidden_states_words, x_rows, v, 1024, 1024, "xc")
+        load_scales(x_scale, hidden_states_scales, 0, PASSES, 1024, 1024, "xsc")
+        for g in range(0, PASSES, 2):
+            load_codes(x_codes, hidden_states_words, g, 2, 1024, 1024, "xc%d" % g)
 
-        def mm(acc, m, c0, width, v):
-            xc, xs = operand(x_table, v, m * P, P)
-            wc, ws = operand(w_table, v, c0, width)
+        def mm(acc, m, c0, width, g):
             nc.tensor.matmul_mx(
                 out=acc[:, 0:width],
-                lhsT=xc.bitcast(FP4X4),
-                lhsT_scale=xs,
-                rhs=wc.bitcast(FP4X4),
-                rhs_scale=ws,
-                start=(v == 0),
-                stop=(v == PASSES - 1),
+                lhsT=window(x_codes, g, m * P, P, 2).bitcast(FP4X4),
+                lhsT_scale=window(x_scale, g, m * P, P, 1),
+                rhs=window(w_codes, g, c0, width, 2).bitcast(FP4X4),
+                rhs_scale=window(w_scale, g, c0, width, 1),
+                start=(g == 0),
+                stop=(g == PASSES - 1),
             )
 
         def evacuate(res, acc, c0, width):
@@ -155,10 +161,10 @@ def tile_gptossmlaattention_pb_kernel(
             for m in range(FIRST_M):
                 acc = psum.tile([P, BANK], F32, name="acc")
                 accs[(m, n)] = acc
-        for v in range(PASSES):
+        for g in range(PASSES):
             for n in range(2):
                 for m in range(FIRST_M):
-                    mm(accs[(m, n)], m, n * BANK, BANK, v)
+                    mm(accs[(m, n)], m, n * BANK, BANK, g)
         for m in range(FIRST_M):
             res = work.tile([P, CHANNELS], F32, name="res")
             ress[m] = res
@@ -169,9 +175,9 @@ def tile_gptossmlaattention_pb_kernel(
         for m in range(FIRST_M):
             acc = psum.tile([P, BANK], F32, name="acc")
             accs[(m, 2)] = acc
-        for v in range(PASSES):
+        for g in range(PASSES):
             for m in range(FIRST_M):
-                mm(accs[(m, 2)], m, 2 * BANK, BANK, v)
+                mm(accs[(m, 2)], m, 2 * BANK, BANK, g)
         for m in range(FIRST_M):
             evacuate(ress[m], accs[(m, 2)], 2 * BANK, BANK)
 
@@ -186,8 +192,8 @@ def tile_gptossmlaattention_pb_kernel(
             res = work.tile([P, CHANNELS], F32, name="res")
             for n in range(3):
                 acc = psum.tile([P, BANK], F32, name="acc")
-                for v in range(PASSES):
-                    mm(acc, m, n * BANK, BANK, v)
+                for g in range(PASSES):
+                    mm(acc, m, n * BANK, BANK, g)
                 evacuate(res, acc, n * BANK, BANK)
             rope(res, m, 0, HEADS)
             store(nc.scalar, res, m, 0, HEADS)
@@ -199,8 +205,8 @@ def tile_gptossmlaattention_pb_kernel(
         )
         for i, (c0, width, h0, h1) in enumerate(tail):
             acc = psum.tile([P, BANK], F32, name="acc")
-            for v in range(PASSES):
-                mm(acc, m, c0, width, v)
+            for g in range(PASSES):
+                mm(acc, m, c0, width, g)
             evacuate(res, acc, c0, width)
             rope(res, m, h0, h1)
             store(nc.sync if i % 2 else nc.scalar, res, m, h0, h1)

@@ -73,6 +73,8 @@ def tile_gptossmlaattention_pb_kernel(
 
         warm = keep.tile([P, BANK], BF16, name="warm")
         nc.gpsimd.memset(warm[:], 0.0)
+        scratch = keep.tile([P, 2], BF16, name="scratch")
+        nc.scalar.copy(out=scratch[:], in_=warm[:, 0:2])
 
         first_tok = FIRST_M * P
         g0 = 0
@@ -87,18 +89,17 @@ def tile_gptossmlaattention_pb_kernel(
                 load_codes(x_codes, hidden_states_words, g, 1, 0, first_tok, "xa%d" % g)
             g0 += npass
 
-        bias = keep.tile([P, CHANNELS], BF16, name="bias")
-        nc.sync.dma_start(out=bias[:], in_=bq.partition_broadcast(P))
-
         load_scales(w_scale, Wq_scales, 0, PASSES, 2 * BANK, BANK, "wsb")
-        load_scales(x_scale, hidden_states_scales, 0, PASSES, 512, 512, "xsb")
         for g in range(0, PASSES, 4):
             load_codes(w_codes, Wq_words, g, 4, 2 * BANK, BANK, "wb%d" % g)
+        load_scales(x_scale, hidden_states_scales, 0, PASSES, 512, 512, "xsb")
         for g in range(0, PASSES, 4):
             load_codes(x_codes, hidden_states_words, g, 4, 512, 512, "xb%d" % g)
 
+        bias = keep.tile([P, CHANNELS], BF16, name="bias")
         cos_t = keep.tile([P, M_TILES, ROPE], BF16, name="cos_t")
         sin_t = keep.tile([P, M_TILES, ROPE], BF16, name="sin_t")
+        nc.sync.dma_start(out=bias[:], in_=bq.partition_broadcast(P))
         nc.sync.dma_start(out=cos_t[:], in_=cos[0].rearrange("(m p) d -> p m d", p=P))
         nc.sync.dma_start(out=sin_t[:], in_=sin[0].rearrange("(m p) d -> p m d", p=P))
 
@@ -157,20 +158,19 @@ def tile_gptossmlaattention_pb_kernel(
 
         accs = {}
         ress = {}
-        for n in range(2):
-            for m in range(FIRST_M):
+        for m in range(FIRST_M):
+            for n in range(2):
                 acc = psum.tile([P, BANK], F32, name="acc")
                 accs[(m, n)] = acc
         for g in range(PASSES):
-            for n in range(2):
-                for m in range(FIRST_M):
+            for m in range(FIRST_M):
+                for n in range(2):
                     mm(accs[(m, n)], m, n * BANK, BANK, g)
         for m in range(FIRST_M):
             res = work.tile([P, CHANNELS], F32, name="res")
             ress[m] = res
-        for n in range(2):
-            for m in range(FIRST_M):
-                evacuate(ress[m], accs[(m, n)], n * BANK, BANK)
+            for n in range(2):
+                nc.scalar.copy(out=res[:, n * BANK : (n + 1) * BANK], in_=accs[(m, n)][:])
 
         for m in range(FIRST_M):
             acc = psum.tile([P, BANK], F32, name="acc")
@@ -179,12 +179,13 @@ def tile_gptossmlaattention_pb_kernel(
             for m in range(FIRST_M):
                 mm(accs[(m, 2)], m, 2 * BANK, BANK, g)
         for m in range(FIRST_M):
-            evacuate(ress[m], accs[(m, 2)], 2 * BANK, BANK)
+            nc.scalar.copy(out=ress[m][:, 2 * BANK : 3 * BANK], in_=accs[(m, 2)][:])
 
         nc.vector.tensor_scalar(
             out=sin_t[:, :, 0:HALF], in0=sin_t[:, :, 0:HALF], scalar1=-1.0, scalar2=None, op0=MULT
         )
         for m in range(FIRST_M):
+            nc.vector.tensor_tensor(out=ress[m][:], in0=ress[m][:], in1=bias[:], op=ADD)
             rope(ress[m], m, 0, HEADS)
             store(nc.scalar, ress[m], m, 0, HEADS)
 

@@ -24,9 +24,10 @@ BANK = 512
 
 FLOPS = 2 * TOKENS * 8192 * CHANNELS
 
-WARM = 10
+WARM = 8
 FIRST_M = 4
-RUNS = (1, 3, 4, 4, 4)
+RUNS = (2, 2, 4, 4, 4)
+LAST = 2 * NOPE
 
 
 def tile_gptossmlaattention_pb_kernel(
@@ -80,10 +81,15 @@ def tile_gptossmlaattention_pb_kernel(
         g0 = 0
         for r, npass in enumerate(RUNS):
             if r == 0:
-                load_codes(w_codes, Wq_words, 0, 1, 0, 2 * BANK, "wa0")
-                load_codes(x_codes, hidden_states_words, 0, 1, 0, first_tok, "xa0")
-            load_scales(x_scale, hidden_states_scales, g0, npass, 0, first_tok, "xsa%d" % r)
-            load_scales(w_scale, Wq_scales, g0, npass, 0, 2 * BANK, "wsa%d" % r)
+                load_codes(x_codes, hidden_states_words, 0, 1, 0, P, "xa0")
+                load_scales(x_scale, hidden_states_scales, g0, npass, 0, first_tok, "xsa%d" % r)
+                load_codes(w_codes, Wq_words, 0, 1, 0, BANK, "wa0")
+                load_scales(w_scale, Wq_scales, g0, npass, 0, 2 * BANK, "wsa%d" % r)
+                load_codes(x_codes, hidden_states_words, 0, 1, P, first_tok - P, "xa0r")
+                load_codes(w_codes, Wq_words, 0, 1, BANK, BANK, "wa0r")
+            else:
+                load_scales(x_scale, hidden_states_scales, g0, npass, 0, first_tok, "xsa%d" % r)
+                load_scales(w_scale, Wq_scales, g0, npass, 0, 2 * BANK, "wsa%d" % r)
             for g in range(max(g0, 1), g0 + npass):
                 load_codes(w_codes, Wq_words, g, 1, 0, 2 * BANK, "wa%d" % g)
                 load_codes(x_codes, hidden_states_words, g, 1, 0, first_tok, "xa%d" % g)
@@ -106,6 +112,21 @@ def tile_gptossmlaattention_pb_kernel(
         load_scales(x_scale, hidden_states_scales, 0, PASSES, 1024, 1024, "xsc")
         for g in range(0, PASSES, 2):
             load_codes(x_codes, hidden_states_words, g, 2, 1024, 1024, "xc%d" % g)
+
+        wn = keep.tile([P, PASSES, 2 * LAST], U8, name="wn", align_bytes=64)
+        wns = keep.tile([P, PASSES, LAST], U8, name="wns", align_bytes=64)
+        nc.vector.memset(wns[:].bitcast(I32), 0)
+        for j in range(2):
+            c0 = (HEADS - 2 + j) * HEAD
+            nc.sync.dma_start(
+                out=wn[:, :, 2 * NOPE * j : 2 * NOPE * (j + 1)].bitcast(I32),
+                in_=Wq_words[:, :, 2 * c0 : 2 * (c0 + NOPE)].rearrange("g p b -> p g b").bitcast(I32),
+            )
+            for q in range(4):
+                nc.sync.dma_start(
+                    out=wns[32 * q : 32 * q + 4, :, NOPE * j : NOPE * (j + 1)].bitcast(I32),
+                    in_=Wq_scales[:, 4 * q : 4 * q + 4, c0 : c0 + NOPE].rearrange("g r n -> r g n").bitcast(I32),
+                )
 
         def mm(acc, m, c0, width, g):
             nc.tensor.matmul_mx(
@@ -162,7 +183,10 @@ def tile_gptossmlaattention_pb_kernel(
             for n in range(2):
                 acc = psum.tile([P, BANK], F32, name="acc")
                 accs[(m, n)] = acc
-        for g in range(PASSES):
+        for n in range(2):
+            for m in range(FIRST_M):
+                mm(accs[(m, n)], m, n * BANK, BANK, 0)
+        for g in range(1, PASSES):
             for m in range(FIRST_M):
                 for n in range(2):
                     mm(accs[(m, n)], m, n * BANK, BANK, g)
@@ -189,6 +213,19 @@ def tile_gptossmlaattention_pb_kernel(
             rope(ress[m], m, 0, HEADS)
             store(nc.scalar, ress[m], m, 0, HEADS)
 
+        mL = M_TILES - 1
+        bias3 = bias[:].rearrange("p (h d) -> p h d", h=HEADS)
+        bb = keep.tile([P, 3, ROPE], F32, name="bb")
+        tb = keep.tile([P, 3, ROPE], F32, name="tb")
+        nc.vector.tensor_tensor(
+            out=tb[:, :, 0:HALF], in0=bias3[:, 5:8, NOPE + HALF : HEAD], in1=spread(sin_t, mL, 0, HALF, 3), op=MULT
+        )
+        nc.vector.tensor_tensor(
+            out=tb[:, :, HALF:ROPE], in0=bias3[:, 5:8, NOPE : NOPE + HALF], in1=spread(sin_t, mL, HALF, ROPE, 3), op=MULT
+        )
+        nc.vector.tensor_tensor(out=bb[:], in0=bias3[:, 5:8, NOPE:HEAD], in1=spread(cos_t, mL, 0, ROPE, 3), op=MULT)
+        nc.vector.tensor_tensor(out=bb[:], in0=bb[:], in1=tb[:], op=ADD)
+
         for m in range(FIRST_M, M_TILES - 1):
             res = work.tile([P, CHANNELS], F32, name="res")
             for n in range(3):
@@ -201,13 +238,49 @@ def tile_gptossmlaattention_pb_kernel(
 
         m = M_TILES - 1
         res = work.tile([P, CHANNELS], F32, name="res")
-        tail = (
-            (0, 512, 0, 2), (512, 256, 2, 4), (768, 256, 4, 5), (1024, 128, 5, 6), (1152, 256, 6, 7), (1408, 128, 7, 8),
-        )
-        for i, (c0, width, h0, h1) in enumerate(tail):
+        res3 = res[:].rearrange("p (h d) -> p h d", h=HEADS)
+        for c0, width, h0, h1 in ((0, 512, 0, 2), (512, 256, 2, 4), (768, 256, 4, 5)):
             acc = psum.tile([P, BANK], F32, name="acc")
             for g in range(PASSES):
                 mm(acc, m, c0, width, g)
             evacuate(res, acc, c0, width)
             rope(res, m, h0, h1)
-            store(nc.sync if i % 2 else nc.scalar, res, m, h0, h1)
+            store(nc.scalar, res, m, h0, h1)
+
+        for h in (5, 6, 7):
+            acc = psum.tile([P, BANK], F32, name="acc")
+            for g in range(PASSES):
+                mm(acc, m, h * HEAD + NOPE, ROPE, g)
+            t = temp.tile([P, ROPE], F32, name="t")
+            u = temp.tile([P, ROPE], F32, name="u")
+            nc.vector.tensor_tensor(out=t[:], in0=acc[:, 0:ROPE], in1=cos_t[:, m, :], op=MULT)
+            nc.vector.tensor_tensor(out=u[:, 0:HALF], in0=acc[:, HALF:ROPE], in1=sin_t[:, m, 0:HALF], op=MULT)
+            nc.vector.tensor_tensor(out=u[:, HALF:ROPE], in0=acc[:, 0:HALF], in1=sin_t[:, m, HALF:ROPE], op=MULT)
+            nc.vector.tensor_tensor(out=t[:], in0=t[:], in1=bb[:, h - 5, :], op=ADD)
+            if h == 5:
+                nc.vector.tensor_tensor(out=res3[:, h, NOPE:HEAD], in0=t[:], in1=u[:], op=ADD)
+                store(nc.sync, res, m, h, h + 1)
+            else:
+                rr = temp.tile([P, ROPE], F32, name="rr")
+                nc.vector.tensor_tensor(out=rr[:], in0=t[:], in1=u[:], op=ADD)
+                queue = nc.scalar if h == 6 else nc.sync
+                queue.dma_start(out=out[0, h, m * P : (m + 1) * P, NOPE:HEAD], in_=rr[:])
+
+        acc = psum.tile([P, BANK], F32, name="acc")
+        for g in range(PASSES):
+            nc.tensor.matmul_mx(
+                out=acc[:, 0:LAST],
+                lhsT=window(x_codes, g, m * P, P, 2).bitcast(FP4X4),
+                lhsT_scale=window(x_scale, g, m * P, P, 1),
+                rhs=wn[:, g, :].bitcast(FP4X4),
+                rhs_scale=wns[:, g, :],
+                start=(g == 0),
+                stop=(g == PASSES - 1),
+            )
+        nn = temp.tile([P, 2, NOPE], F32, name="nn")
+        nc.vector.tensor_tensor(
+            out=nn[:], in0=acc[:, 0:LAST].rearrange("p (h d) -> p h d", h=2), in1=bias3[:, HEADS - 2 : HEADS, 0:NOPE], op=ADD
+        )
+        nc.scalar.dma_start(
+            out=out[0, HEADS - 2 : HEADS, m * P : (m + 1) * P, 0:NOPE].rearrange("h p d -> p h d"), in_=nn[:]
+        )

@@ -27,7 +27,7 @@ FLOPS = 2 * TOKENS * 8192 * CHANNELS
 WARM = 8
 FIRST_M = 4
 RUNS = (2, 2, 4, 4, 4)
-LAST = 2 * NOPE
+TAIL = 256
 
 
 def tile_gptossmlaattention_pb_kernel(
@@ -46,14 +46,20 @@ def tile_gptossmlaattention_pb_kernel(
         w_codes = [[] for g in range(PASSES)]
         w_scale = [[] for g in range(PASSES)]
 
-        def load_codes(table, src, g0, npass, c0, ncols, name):
+        def code_tile(npass, ncols, name):
             t = keep.tile([P, npass, 2 * ncols], U8, name=name, align_bytes=64)
+            return t
+
+        def fill_codes(table, src, g0, npass, c0, ncols, t, slot):
             nc.sync.dma_start(
-                out=t[:].bitcast(I32),
+                out=t[:, slot : slot + npass, :].bitcast(I32),
                 in_=src[g0 : g0 + npass, :, 2 * c0 : 2 * (c0 + ncols)].rearrange("g p b -> p g b").bitcast(I32),
             )
             for j in range(npass):
-                table[g0 + j].append((c0, c0 + ncols, t[:, j, :]))
+                table[g0 + j].append((c0, c0 + ncols, t[:, slot + j, :]))
+
+        def load_codes(table, src, g0, npass, c0, ncols, name):
+            fill_codes(table, src, g0, npass, c0, ncols, code_tile(npass, ncols, name), 0)
 
         def load_scales(table, src, g0, npass, c0, ncols, name):
             t = keep.tile([P, npass, ncols], U8, name=name, align_bytes=64)
@@ -92,7 +98,12 @@ def tile_gptossmlaattention_pb_kernel(
                 load_scales(w_scale, Wq_scales, g0, npass, 0, 2 * BANK, "wsa%d" % r)
             for g in range(max(g0, 1), g0 + npass):
                 load_codes(w_codes, Wq_words, g, 1, 0, 2 * BANK, "wa%d" % g)
-                load_codes(x_codes, hidden_states_words, g, 1, 0, first_tok, "xa%d" % g)
+                if g < 4:
+                    load_codes(x_codes, hidden_states_words, g, 1, 0, first_tok, "xa%d" % g)
+                else:
+                    if g % 4 == 0:
+                        quad = code_tile(4, first_tok, "xq%d" % g)
+                    fill_codes(x_codes, hidden_states_words, g, 1, 0, first_tok, quad, g % 4)
             g0 += npass
 
         load_scales(w_scale, Wq_scales, 0, PASSES, 2 * BANK, BANK, "wsb")
@@ -100,7 +111,9 @@ def tile_gptossmlaattention_pb_kernel(
             load_codes(w_codes, Wq_words, g, 4, 2 * BANK, BANK, "wb%d" % g)
         load_scales(x_scale, hidden_states_scales, 0, PASSES, 512, 512, "xsb")
         for g in range(0, PASSES, 4):
-            load_codes(x_codes, hidden_states_words, g, 4, 512, 512, "xb%d" % g)
+            if g % 8 == 0:
+                octet = code_tile(8, 512, "xb%d" % g)
+            fill_codes(x_codes, hidden_states_words, g, 4, 512, 512, octet, g % 8)
 
         bias = keep.tile([P, CHANNELS], BF16, name="bias")
         cos_t = keep.tile([P, M_TILES, ROPE], BF16, name="cos_t")
@@ -112,21 +125,6 @@ def tile_gptossmlaattention_pb_kernel(
         load_scales(x_scale, hidden_states_scales, 0, PASSES, 1024, 1024, "xsc")
         for g in range(0, PASSES, 2):
             load_codes(x_codes, hidden_states_words, g, 2, 1024, 1024, "xc%d" % g)
-
-        wn = keep.tile([P, PASSES, 2 * LAST], U8, name="wn", align_bytes=64)
-        wns = keep.tile([P, PASSES, LAST], U8, name="wns", align_bytes=64)
-        nc.vector.memset(wns[:].bitcast(I32), 0)
-        for j in range(2):
-            c0 = (HEADS - 2 + j) * HEAD
-            nc.sync.dma_start(
-                out=wn[:, :, 2 * NOPE * j : 2 * NOPE * (j + 1)].bitcast(I32),
-                in_=Wq_words[:, :, 2 * c0 : 2 * (c0 + NOPE)].rearrange("g p b -> p g b").bitcast(I32),
-            )
-            for q in range(4):
-                nc.sync.dma_start(
-                    out=wns[32 * q : 32 * q + 4, :, NOPE * j : NOPE * (j + 1)].bitcast(I32),
-                    in_=Wq_scales[:, 4 * q : 4 * q + 4, c0 : c0 + NOPE].rearrange("g r n -> r g n").bitcast(I32),
-                )
 
         def mm(acc, m, c0, width, g):
             nc.tensor.matmul_mx(
@@ -215,17 +213,19 @@ def tile_gptossmlaattention_pb_kernel(
 
         mL = M_TILES - 1
         bias3 = bias[:].rearrange("p (h d) -> p h d", h=HEADS)
-        bb = keep.tile([P, 3, ROPE], F32, name="bb")
-        tb = keep.tile([P, 3, ROPE], F32, name="tb")
+        bb = keep.tile([P, 4, ROPE], F32, name="bb")
+        tb = keep.tile([P, 4, ROPE], F32, name="tb")
         nc.vector.tensor_tensor(
-            out=tb[:, :, 0:HALF], in0=bias3[:, 5:8, NOPE + HALF : HEAD], in1=spread(sin_t, mL, 0, HALF, 3), op=MULT
+            out=tb[:, :, 0:HALF], in0=bias3[:, 4:8, NOPE + HALF : HEAD], in1=spread(sin_t, mL, 0, HALF, 4), op=MULT
         )
         nc.vector.tensor_tensor(
-            out=tb[:, :, HALF:ROPE], in0=bias3[:, 5:8, NOPE : NOPE + HALF], in1=spread(sin_t, mL, HALF, ROPE, 3), op=MULT
+            out=tb[:, :, HALF:ROPE], in0=bias3[:, 4:8, NOPE : NOPE + HALF], in1=spread(sin_t, mL, HALF, ROPE, 4), op=MULT
         )
-        nc.vector.tensor_tensor(out=bb[:], in0=bias3[:, 5:8, NOPE:HEAD], in1=spread(cos_t, mL, 0, ROPE, 3), op=MULT)
+        nc.vector.tensor_tensor(out=bb[:], in0=bias3[:, 4:8, NOPE:HEAD], in1=spread(cos_t, mL, 0, ROPE, 4), op=MULT)
         nc.vector.tensor_tensor(out=bb[:], in0=bb[:], in1=tb[:], op=ADD)
 
+        tail_codes = []
+        tail_scale = []
         for m in range(FIRST_M, M_TILES - 1):
             res = work.tile([P, CHANNELS], F32, name="res")
             for n in range(3):
@@ -235,11 +235,30 @@ def tile_gptossmlaattention_pb_kernel(
                 evacuate(res, acc, n * BANK, BANK)
             rope(res, m, 0, HEADS)
             store(nc.scalar, res, m, 0, HEADS)
+            if m == 7:
+                for cname, sname, width, d0, heads in (
+                    ("xb0", "xq4", ROPE, NOPE, (4, 5)), ("xb8", "xq8", ROPE, NOPE, (6, 7)), ("xsb", "xq12", NOPE, 0, (4, 5, 6, 7)),
+                ):
+                    ct = keep.tile([P, PASSES, 2 * TAIL], U8, name=cname, align_bytes=64)
+                    st = keep.tile([P, PASSES, TAIL], U8, name=sname, align_bytes=64)
+                    nc.vector.memset(st[:].bitcast(I32), 0)
+                    for j, h in enumerate(heads):
+                        c0 = h * HEAD + d0
+                        nc.sync.dma_start(
+                            out=ct[:, :, 2 * width * j : 2 * width * (j + 1)].bitcast(I32),
+                            in_=Wq_words[:, :, 2 * c0 : 2 * (c0 + width)].rearrange("g p b -> p g b").bitcast(I32),
+                        )
+                        for q in range(4):
+                            nc.sync.dma_start(
+                                out=st[32 * q : 32 * q + 4, :, width * j : width * (j + 1)].bitcast(I32),
+                                in_=Wq_scales[:, 4 * q : 4 * q + 4, c0 : c0 + width].rearrange("g r n -> r g n").bitcast(I32),
+                            )
+                    tail_codes.append(ct)
+                    tail_scale.append(st)
 
         m = M_TILES - 1
         res = work.tile([P, CHANNELS], F32, name="res")
-        res3 = res[:].rearrange("p (h d) -> p h d", h=HEADS)
-        for c0, width, h0, h1 in ((0, 512, 0, 2), (512, 256, 2, 4), (768, 256, 4, 5)):
+        for c0, width, h0, h1 in ((0, 512, 0, 2), (512, 256, 2, 4)):
             acc = psum.tile([P, BANK], F32, name="acc")
             for g in range(PASSES):
                 mm(acc, m, c0, width, g)
@@ -247,40 +266,39 @@ def tile_gptossmlaattention_pb_kernel(
             rope(res, m, h0, h1)
             store(nc.scalar, res, m, h0, h1)
 
-        for h in (5, 6, 7):
+        def tail_group(k):
             acc = psum.tile([P, BANK], F32, name="acc")
             for g in range(PASSES):
-                mm(acc, m, h * HEAD + NOPE, ROPE, g)
-            t = temp.tile([P, ROPE], F32, name="t")
-            u = temp.tile([P, ROPE], F32, name="u")
-            nc.vector.tensor_tensor(out=t[:], in0=acc[:, 0:ROPE], in1=cos_t[:, m, :], op=MULT)
-            nc.vector.tensor_tensor(out=u[:, 0:HALF], in0=acc[:, HALF:ROPE], in1=sin_t[:, m, 0:HALF], op=MULT)
-            nc.vector.tensor_tensor(out=u[:, HALF:ROPE], in0=acc[:, 0:HALF], in1=sin_t[:, m, HALF:ROPE], op=MULT)
-            nc.vector.tensor_tensor(out=t[:], in0=t[:], in1=bb[:, h - 5, :], op=ADD)
-            if h == 5:
-                nc.vector.tensor_tensor(out=res3[:, h, NOPE:HEAD], in0=t[:], in1=u[:], op=ADD)
-                store(nc.sync, res, m, h, h + 1)
-            else:
-                rr = temp.tile([P, ROPE], F32, name="rr")
-                nc.vector.tensor_tensor(out=rr[:], in0=t[:], in1=u[:], op=ADD)
-                queue = nc.scalar if h == 6 else nc.sync
-                queue.dma_start(out=out[0, h, m * P : (m + 1) * P, NOPE:HEAD], in_=rr[:])
+                nc.tensor.matmul_mx(
+                    out=acc[:, 0:TAIL],
+                    lhsT=window(x_codes, g, m * P, P, 2).bitcast(FP4X4),
+                    lhsT_scale=window(x_scale, g, m * P, P, 1),
+                    rhs=tail_codes[k][:, g, :].bitcast(FP4X4),
+                    rhs_scale=tail_scale[k][:, g, :],
+                    start=(g == 0),
+                    stop=(g == PASSES - 1),
+                )
+            return acc
 
-        acc = psum.tile([P, BANK], F32, name="acc")
-        for g in range(PASSES):
-            nc.tensor.matmul_mx(
-                out=acc[:, 0:LAST],
-                lhsT=window(x_codes, g, m * P, P, 2).bitcast(FP4X4),
-                lhsT_scale=window(x_scale, g, m * P, P, 1),
-                rhs=wn[:, g, :].bitcast(FP4X4),
-                rhs_scale=wns[:, g, :],
-                start=(g == 0),
-                stop=(g == PASSES - 1),
+        for k in range(2):
+            acc = tail_group(k)
+            acc3 = acc[:, 0:TAIL].rearrange("p (h d) -> p h d", h=2)
+            t = temp.tile([P, 2, ROPE], F32, name="t")
+            u = temp.tile([P, 2, ROPE], F32, name="u")
+            rr = temp.tile([P, 2, ROPE], F32, name="rr")
+            nc.vector.tensor_tensor(out=t[:], in0=acc3, in1=spread(cos_t, m, 0, ROPE, 2), op=MULT)
+            nc.vector.tensor_tensor(out=u[:, :, 0:HALF], in0=acc3[:, :, HALF:ROPE], in1=spread(sin_t, m, 0, HALF, 2), op=MULT)
+            nc.vector.tensor_tensor(out=u[:, :, HALF:ROPE], in0=acc3[:, :, 0:HALF], in1=spread(sin_t, m, HALF, ROPE, 2), op=MULT)
+            nc.vector.tensor_tensor(out=t[:], in0=t[:], in1=bb[:, 2 * k : 2 * k + 2, :], op=ADD)
+            nc.vector.tensor_tensor(out=rr[:], in0=t[:], in1=u[:], op=ADD)
+            queue = nc.sync if k == 0 else nc.scalar
+            queue.dma_start(
+                out=out[0, 4 + 2 * k : 6 + 2 * k, m * P : (m + 1) * P, NOPE:HEAD].rearrange("h p d -> p h d"), in_=rr[:]
             )
-        nn = temp.tile([P, 2, NOPE], F32, name="nn")
+
+        acc = tail_group(2)
+        nn = temp.tile([P, 4, NOPE], F32, name="nn")
         nc.vector.tensor_tensor(
-            out=nn[:], in0=acc[:, 0:LAST].rearrange("p (h d) -> p h d", h=2), in1=bias3[:, HEADS - 2 : HEADS, 0:NOPE], op=ADD
+            out=nn[:], in0=acc[:, 0:TAIL].rearrange("p (h d) -> p h d", h=4), in1=bias3[:, 4:8, 0:NOPE], op=ADD
         )
-        nc.scalar.dma_start(
-            out=out[0, HEADS - 2 : HEADS, m * P : (m + 1) * P, 0:NOPE].rearrange("h p d -> p h d"), in_=nn[:]
-        )
+        nc.sync.dma_start(out=out[0, 4:8, m * P : (m + 1) * P, 0:NOPE].rearrange("h p d -> p h d"), in_=nn[:])

@@ -47,7 +47,7 @@ def tile_gptossmlaattention_pb_kernel(
         w_scale = [[] for g in range(PASSES)]
 
         def code_tile(npass, ncols, name):
-            t = keep.tile([P, npass, 2 * ncols], U8, name=name, align_bytes=64)
+            t = keep.tile([P, npass, 2 * ncols], U8, name=name, align_bytes=256)
             return t
 
         def fill_codes(table, src, g0, npass, c0, ncols, t, slot):
@@ -62,7 +62,7 @@ def tile_gptossmlaattention_pb_kernel(
             fill_codes(table, src, g0, npass, c0, ncols, code_tile(npass, ncols, name), 0)
 
         def load_scales(table, src, g0, npass, c0, ncols, name):
-            t = keep.tile([P, npass, ncols], U8, name=name, align_bytes=64)
+            t = keep.tile([P, npass, ncols], U8, name=name, align_bytes=256)
             nc.vector.memset(t[:].bitcast(I32), 0)
             for q in range(4):
                 nc.sync.dma_start(
@@ -78,7 +78,7 @@ def tile_gptossmlaattention_pb_kernel(
                     return t[:, unit * (c0 - a) : unit * (c0 - a + width)]
             return None
 
-        warm = keep.tile([P, BANK], BF16, name="warm")
+        warm = keep.tile([P, BANK], BF16, name="warm", align_bytes=256)
         nc.gpsimd.memset(warm[:], 0.0)
         scratch = keep.tile([P, 2], BF16, name="scratch")
         nc.scalar.copy(out=scratch[:], in_=warm[:, 0:2])
@@ -239,8 +239,8 @@ def tile_gptossmlaattention_pb_kernel(
                 for cname, sname, width, d0, heads in (
                     ("xb0", "xq4", ROPE, NOPE, (4, 5)), ("xb8", "xq8", ROPE, NOPE, (6, 7)), ("xsb", "xq12", NOPE, 0, (4, 5, 6, 7)),
                 ):
-                    ct = keep.tile([P, PASSES, 2 * TAIL], U8, name=cname, align_bytes=64)
-                    st = keep.tile([P, PASSES, TAIL], U8, name=sname, align_bytes=64)
+                    ct = keep.tile([P, PASSES, 2 * TAIL], U8, name=cname, align_bytes=256)
+                    st = keep.tile([P, PASSES, TAIL], U8, name=sname, align_bytes=256)
                     nc.vector.memset(st[:].bitcast(I32), 0)
                     for j, h in enumerate(heads):
                         c0 = h * HEAD + d0
@@ -297,7 +297,7 @@ def tile_gptossmlaattention_pb_kernel(
             )
 
         acc = tail_group(2)
-        nn = temp.tile([P, 4, NOPE], F32, name="nn")
+        nn = temp.tile([P, 4, NOPE], F32, name="rr")
         nc.vector.tensor_tensor(
             out=nn[:], in0=acc[:, 0:TAIL].rearrange("p (h d) -> p h d", h=4), in1=bias3[:, 4:8, 0:NOPE], op=ADD
         )

@@ -64,10 +64,10 @@ def tile_gptossmlaattention_pb_kernel(
         def load_scales(table, src, g0, npass, c0, ncols, name):
             t = keep.tile([P, npass, ncols], U8, name=name, align_bytes=256)
             nc.vector.memset(t[:].bitcast(I32), 0)
-            for q in range(4):
+            for r in range(4):
                 nc.sync.dma_start(
-                    out=t[32 * q : 32 * q + 4, :, :].bitcast(I32),
-                    in_=src[g0 : g0 + npass, 4 * q : 4 * q + 4, c0 : c0 + ncols].rearrange("g r n -> r g n").bitcast(I32),
+                    out=t[r : P : 32, :, :].bitcast(I32),
+                    in_=src[g0 : g0 + npass, r : 16 : 4, c0 : c0 + ncols].rearrange("g q n -> q g n").bitcast(I32),
                 )
             for j in range(npass):
                 table[g0 + j].append((c0, c0 + ncols, t[:, j, :]))

from contextlib import ExitStack

import concourse.mybir as mybir

F32 = mybir.dt.float32
BF16 = mybir.dt.bfloat16
I32 = mybir.dt.int32
U8 = mybir.dt.uint8
FP4X4 = mybir.dt.float4_e2m1fn_x4
ADD = mybir.AluOpType.add
MULT = mybir.AluOpType.mult

P = 128
PASSES = 16
TOKENS = 2048
CHANNELS = 1536
HEADS = 8
HEAD = 192
NOPE = 64
ROPE = 128
HALF = 64
M_TILES = TOKENS // P
BANK = 512

FLOPS = 2 * TOKENS * 8192 * CHANNELS

WARM = 8
FIRST_M = 4
RUNS = (2, 2, 4, 4, 4)
TAIL = 256


def tile_gptossmlaattention_pb_kernel(
    tc, hidden_states_words, hidden_states_scales, cos, sin, Wq_words, Wq_scales, bq, out
):
    nc = tc.nc
    with ExitStack() as ctx:
        keep = ctx.enter_context(tc.tile_pool(name="keep", bufs=1))
        work = ctx.enter_context(tc.tile_pool(name="work", bufs=5))
        temp = ctx.enter_context(tc.tile_pool(name="temp", bufs=2))
        psum = ctx.enter_context(tc.psum_pool(name="psum", bufs=8))
        ctx.enter_context(tc.manual_schedule())

        x_codes = [[] for g in range(PASSES)]
        x_scale = [[] for g in range(PASSES)]
        w_codes = [[] for g in range(PASSES)]
        w_scale = [[] for g in range(PASSES)]

        def code_tile(npass, ncols, name):
            t = keep.tile([P, npass, 2 * ncols], U8, name=name, align_bytes=256)
            return t

        def fill_codes(table, src, g0, npass, c0, ncols, t, slot):
            nc.sync.dma_start(
                out=t[:, slot : slot + npass, :].bitcast(I32),
                in_=src[g0 : g0 + npass, :, 2 * c0 : 2 * (c0 + ncols)].rearrange("g p b -> p g b").bitcast(I32),
            )
            for j in range(npass):
                table[g0 + j].append((c0, c0 + ncols, t[:, slot + j, :]))

        def load_codes(table, src, g0, npass, c0, ncols, name):
            fill_codes(table, src, g0, npass, c0, ncols, code_tile(npass, ncols, name), 0)

        def load_scales(table, src, g0, npass, c0, ncols, name):
            t = keep.tile([P, npass, ncols], U8, name=name, align_bytes=256)
            nc.vector.memset(t[:].bitcast(I32), 0)
            for r in range(4):
                nc.sync.dma_start(
                    out=t[r : P : 32, :, :].bitcast(I32),
                    in_=src[g0 : g0 + npass, r : 16 : 4, c0 : c0 + ncols].rearrange("g q n -> q g n").bitcast(I32),
                )
            for j in range(npass):
                table[g0 + j].append((c0, c0 + ncols, t[:, j, :]))

        def window(table, g, c0, width, unit):
            for a, b, t in table[g]:
                if a <= c0 and c0 + width <= b:
                    return t[:, unit * (c0 - a) : unit * (c0 - a + width)]
            return None

        warm = keep.tile([P, BANK], BF16, name="warm", align_bytes=256)
        nc.gpsimd.memset(warm[:], 0.0)
        scratch = keep.tile([P, 2], BF16, name="scratch")
        nc.scalar.copy(out=scratch[:], in_=warm[:, 0:2])

        first_tok = FIRST_M * P
        g0 = 0
        for r, npass in enumerate(RUNS):
            if r == 0:
                load_codes(x_codes, hidden_states_words, 0, 1, 0, P, "xa0")
                load_scales(x_scale, hidden_states_scales, g0, npass, 0, first_tok, "xsa%d" % r)
                load_codes(w_codes, Wq_words, 0, 1, 0, BANK, "wa0")
                load_scales(w_scale, Wq_scales, g0, npass, 0, 2 * BANK, "wsa%d" % r)
                load_codes(x_codes, hidden_states_words, 0, 1, P, first_tok - P, "xa0r")
                load_codes(w_codes, Wq_words, 0, 1, BANK, BANK, "wa0r")
            else:
                load_scales(x_scale, hidden_states_scales, g0, npass, 0, first_tok, "xsa%d" % r)
                load_scales(w_scale, Wq_scales, g0, npass, 0, 2 * BANK, "wsa%d" % r)
            for g in range(max(g0, 1), g0 + npass):
                load_codes(w_codes, Wq_words, g, 1, 0, 2 * BANK, "wa%d" % g)
                if g < 4:
                    load_codes(x_codes, hidden_states_words, g, 1, 0, first_tok, "xa%d" % g)
                else:
                    if g % 4 == 0:
                        quad = code_tile(4, first_tok, "xq%d" % g)
                    fill_codes(x_codes, hidden_states_words, g, 1, 0, first_tok, quad, g % 4)
            g0 += npass

        load_scales(w_scale, Wq_scales, 0, PASSES, 2 * BANK, BANK, "wsb")
        for g in range(0, PASSES, 4):
            load_codes(w_codes, Wq_words, g, 4, 2 * BANK, BANK, "wb%d" % g)
        load_scales(x_scale, hidden_states_scales, 0, PASSES, 512, 512, "xsb")
        for g in range(0, PASSES, 4):
            if g % 8 == 0:
                octet = code_tile(8, 512, "xb%d" % g)
            fill_codes(x_codes, hidden_states_words, g, 4, 512, 512, octet, g % 8)

        bias = keep.tile([P, CHANNELS], BF16, name="bias")
        cos_t = keep.tile([P, M_TILES, ROPE], BF16, name="cos_t")
        sin_t = keep.tile([P, M_TILES, ROPE], BF16, name="sin_t")
        nc.sync.dma_start(out=bias[:], in_=bq.partition_broadcast(P))
        nc.sync.dma_start(out=cos_t[:], in_=cos[0].rearrange("(m p) d -> p m d", p=P))
        nc.sync.dma_start(out=sin_t[:], in_=sin[0].rearrange("(m p) d -> p m d", p=P))

        load_scales(x_scale, hidden_states_scales, 0, PASSES, 1024, 1024, "xsc")
        for g in range(0, PASSES, 2):
            load_codes(x_codes, hidden_states_words, g, 2, 1024, 1024, "xc%d" % g)

        def mm(acc, m, c0, width, g):
            nc.tensor.matmul_mx(
                out=acc[:, 0:width],
                lhsT=window(x_codes, g, m * P, P, 2).bitcast(FP4X4),
                lhsT_scale=window(x_scale, g, m * P, P, 1),
                rhs=window(w_codes, g, c0, width, 2).bitcast(FP4X4),
                rhs_scale=window(w_scale, g, c0, width, 1),
                start=(g == 0),
                stop=(g == PASSES - 1),
            )

        def evacuate(res, acc, c0, width):
            nc.vector.tensor_tensor(
                out=res[:, c0 : c0 + width], in0=acc[:, 0:width], in1=bias[:, c0 : c0 + width], op=ADD
            )

        def spread(table, m, d0, d1, nh):
            return table[:, m, d0:d1].unsqueeze(1).to_broadcast([P, nh, d1 - d0])

        def rope(res, m, h0, h1):
            nh = h1 - h0
            res3 = res[:].rearrange("p (h d) -> p h d", h=HEADS)
            tmp = temp.tile([P, HEADS, ROPE], F32, name="tmp")
            nc.vector.tensor_tensor(
                out=tmp[:, h0:h1, 0:HALF], in0=res3[:, h0:h1, NOPE + HALF : HEAD],
                in1=spread(sin_t, m, 0, HALF, nh), op=MULT,
            )
            nc.vector.tensor_tensor(
                out=tmp[:, h0:h1, HALF:ROPE], in0=res3[:, h0:h1, NOPE : NOPE + HALF],
                in1=spread(sin_t, m, HALF, ROPE, nh), op=MULT,
            )
            nc.vector.tensor_tensor(
                out=res3[:, h0:h1, NOPE:HEAD], in0=res3[:, h0:h1, NOPE:HEAD],
                in1=spread(cos_t, m, 0, ROPE, nh), op=MULT,
            )
            nc.vector.tensor_tensor(
                out=res3[:, h0:h1, NOPE:HEAD], in0=res3[:, h0:h1, NOPE:HEAD], in1=tmp[:, h0:h1, :], op=ADD
            )

        def store(queue, res, m, h0, h1):
            res3 = res[:].rearrange("p (h d) -> p h d", h=HEADS)
            queue.dma_start(
                out=out[0, h0:h1, m * P : (m + 1) * P, :].rearrange("h p d -> p h d"), in_=res3[:, h0:h1, :]
            )

        dummy = psum.tile([P, BANK], F32, name="acc")
        for i in range(WARM):
            nc.tensor.matmul(out=dummy[:], lhsT=warm[:, 0:P], rhs=warm[:], start=True, stop=True)

        accs = {}
        ress = {}
        for m in range(FIRST_M):
            for n in range(2):
                acc = psum.tile([P, BANK], F32, name="acc")
                accs[(m, n)] = acc
        for n in range(2):
            for m in range(FIRST_M):
                mm(accs[(m, n)], m, n * BANK, BANK, 0)
        for g in range(1, PASSES):
            for m in range(FIRST_M):
                for n in range(2):
                    mm(accs[(m, n)], m, n * BANK, BANK, g)
        for m in range(FIRST_M):
            res = work.tile([P, CHANNELS], F32, name="res")
            ress[m] = res
            for n in range(2):
                nc.scalar.copy(out=res[:, n * BANK : (n + 1) * BANK], in_=accs[(m, n)][:])

        for m in range(FIRST_M):
            acc = psum.tile([P, BANK], F32, name="acc")
            accs[(m, 2)] = acc
        for g in range(PASSES):
            for m in range(FIRST_M):
                mm(accs[(m, 2)], m, 2 * BANK, BANK, g)
        for m in range(FIRST_M):
            nc.scalar.copy(out=ress[m][:, 2 * BANK : 3 * BANK], in_=accs[(m, 2)][:])

        nc.vector.tensor_scalar(
            out=sin_t[:, :, 0:HALF], in0=sin_t[:, :, 0:HALF], scalar1=-1.0, scalar2=None, op0=MULT
        )
        for m in range(FIRST_M):
            nc.vector.tensor_tensor(out=ress[m][:], in0=ress[m][:], in1=bias[:], op=ADD)
            rope(ress[m], m, 0, HEADS)
            store(nc.scalar, ress[m], m, 0, HEADS)

        mL = M_TILES - 1
        bias3 = bias[:].rearrange("p (h d) -> p h d", h=HEADS)
        bb = keep.tile([P, 4, ROPE], F32, name="bb")
        tb = keep.tile([P, 4, ROPE], F32, name="tb")
        nc.vector.tensor_tensor(
            out=tb[:, :, 0:HALF], in0=bias3[:, 4:8, NOPE + HALF : HEAD], in1=spread(sin_t, mL, 0, HALF, 4), op=MULT
        )
        nc.vector.tensor_tensor(
            out=tb[:, :, HALF:ROPE], in0=bias3[:, 4:8, NOPE : NOPE + HALF], in1=spread(sin_t, mL, HALF, ROPE, 4), op=MULT
        )
        nc.vector.tensor_tensor(out=bb[:], in0=bias3[:, 4:8, NOPE:HEAD], in1=spread(cos_t, mL, 0, ROPE, 4), op=MULT)
        nc.vector.tensor_tensor(out=bb[:], in0=bb[:], in1=tb[:], op=ADD)

        tail_codes = []
        tail_scale = []
        for m in range(FIRST_M, M_TILES - 1):
            res = work.tile([P, CHANNELS], F32, name="res")
            for n in range(3):
                acc = psum.tile([P, BANK], F32, name="acc")
                for g in range(PASSES):
                    mm(acc, m, n * BANK, BANK, g)
                evacuate(res, acc, n * BANK, BANK)
            rope(res, m, 0, HEADS)
            store(nc.scalar, res, m, 0, HEADS)
            if m == 7:
                for cname, sname, width, d0, heads in (
                    ("xb0", "xq4", ROPE, NOPE, (4, 5)), ("xb8", "xq8", ROPE, NOPE, (6, 7)), ("xsb", "xq12", NOPE, 0, (4, 5, 6, 7)),
                ):
                    ct = keep.tile([P, PASSES, 2 * TAIL], U8, name=cname, align_bytes=256)
                    st = keep.tile([P, PASSES, TAIL], U8, name=sname, align_bytes=256)
                    nc.vector.memset(st[:].bitcast(I32), 0)
                    for j, h in enumerate(heads):
                        c0 = h * HEAD + d0
                        nc.sync.dma_start(
                            out=ct[:, :, 2 * width * j : 2 * width * (j + 1)].bitcast(I32),
                            in_=Wq_words[:, :, 2 * c0 : 2 * (c0 + width)].rearrange("g p b -> p g b").bitcast(I32),
                        )
                        for q in range(4):
                            nc.sync.dma_start(
                                out=st[32 * q : 32 * q + 4, :, width * j : width * (j + 1)].bitcast(I32),
                                in_=Wq_scales[:, 4 * q : 4 * q + 4, c0 : c0 + width].rearrange("g r n -> r g n").bitcast(I32),
                            )
                    tail_codes.append(ct)
                    tail_scale.append(st)

        m = M_TILES - 1
        res = work.tile([P, CHANNELS], F32, name="res")
        for c0, width, h0, h1 in ((0, 512, 0, 2), (512, 256, 2, 4)):
            acc = psum.tile([P, BANK], F32, name="acc")
            for g in range(PASSES):
                mm(acc, m, c0, width, g)
            evacuate(res, acc, c0, width)
            rope(res, m, h0, h1)
            store(nc.scalar, res, m, h0, h1)

        def tail_group(k):
            acc = psum.tile([P, BANK], F32, name="acc")
            for g in range(PASSES):
                nc.tensor.matmul_mx(
                    out=acc[:, 0:TAIL],
                    lhsT=window(x_codes, g, m * P, P, 2).bitcast(FP4X4),
                    lhsT_scale=window(x_scale, g, m * P, P, 1),
                    rhs=tail_codes[k][:, g, :].bitcast(FP4X4),
                    rhs_scale=tail_scale[k][:, g, :],
                    start=(g == 0),
                    stop=(g == PASSES - 1),
                )
            return acc

        for k in range(2):
            acc = tail_group(k)
            acc3 = acc[:, 0:TAIL].rearrange("p (h d) -> p h d", h=2)
            t = temp.tile([P, 2, ROPE], F32, name="t")
            u = temp.tile([P, 2, ROPE], F32, name="u")
            rr = temp.tile([P, 2, ROPE], F32, name="rr")
            nc.vector.tensor_tensor(out=t[:], in0=acc3, in1=spread(cos_t, m, 0, ROPE, 2), op=MULT)
            nc.vector.tensor_tensor(out=u[:, :, 0:HALF], in0=acc3[:, :, HALF:ROPE], in1=spread(sin_t, m, 0, HALF, 2), op=MULT)
            nc.vector.tensor_tensor(out=u[:, :, HALF:ROPE], in0=acc3[:, :, 0:HALF], in1=spread(sin_t, m, HALF, ROPE, 2), op=MULT)
            nc.vector.tensor_tensor(out=t[:], in0=t[:], in1=bb[:, 2 * k : 2 * k + 2, :], op=ADD)
            nc.vector.tensor_tensor(out=rr[:], in0=t[:], in1=u[:], op=ADD)
            queue = nc.sync if k == 0 else nc.scalar
            queue.dma_start(
                out=out[0, 4 + 2 * k : 6 + 2 * k, m * P : (m + 1) * P, NOPE:HEAD].rearrange("h p d -> p h d"), in_=rr[:]
            )

        acc = tail_group(2)
        nn = temp.tile([P, 4, NOPE], F32, name="rr")
        nc.vector.tensor_tensor(
            out=nn[:], in0=acc[:, 0:TAIL].rearrange("p (h d) -> p h d", h=4), in1=bias3[:, 4:8, 0:NOPE], op=ADD
        )
        nc.sync.dma_start(out=out[0, 4:8, m * P : (m + 1) * P, 0:NOPE].rearrange("h p d -> p h d"), in_=nn[:])
